import numpy as np
import ml_dtypes

BF16 = ml_dtypes.bfloat16


def bf(x):
    return np.asarray(x, np.float32).astype(BF16)


def f32(x):
    return np.asarray(x, np.float32)


def f64(x):
    return np.asarray(x).astype(np.float64)


def striped(idx):
    return np.tile(idx.reshape(-1, 16).T, (8, 1))


C, S, N, K = 1024, 1024, 1024, 128


def setup_inputs():
    table = f32(np.random.standard_normal((C, S)))
    vulns = f32(np.random.standard_normal((K, N)) * (0.5 + np.random.random((1, N))) / np.sqrt(K))
    return {"table": table, "vulns": vulns, "offs": striped(np.random.permutation(S)[:N])}


def reference(table, vulns, offs):
    idx = offs[:16].T.reshape(-1)
    amp = np.sqrt(np.sum(f64(vulns) ** 2, axis=0, keepdims=True))
    return f64(table)[:, idx] * amp

@@ -1,0 +1,48 @@
+import concourse.mybir as mybir
+
+F32, BF16, U16 = mybir.dt.float32, mybir.dt.bfloat16, mybir.dt.uint16
+MULT = mybir.AluOpType.mult
+SQRT = mybir.ActivationFunctionType.Sqrt
+
+P = 128
+BANK = 512
+
+FLOPS = 2 * 128 * 1024 + 1024 * 1024
+
+
+def tile_omegaentangle_kernel(tc, table, vulns, offs, out):
+    nc = tc.nc
+    C, S = table.shape
+    K, N = vulns.shape
+    blocks = C // P
+
+    with (
+        tc.tile_pool(name="held", bufs=1) as held,
+        tc.tile_pool(name="windows", bufs=blocks) as windows,
+        tc.tile_pool(name="products", bufs=blocks) as products,
+        tc.psum_pool(name="psum", bufs=N // BANK) as psum,
+    ):
+        offsets = held.tile([P, N // 16], U16, name="offsets")
+        nc.sync.dma_start(offsets[:], offs)
+
+        components = held.tile([K, N], F32, name="components")
+        nc.scalar.dma_start(components[:], vulns)
+
+        ones = held.tile([K, P], BF16, name="ones")
+        nc.gpsimd.memset(ones[:], 1.0)
+        squares = held.tile([K, N], BF16, name="squares")
+        nc.vector.tensor_tensor(squares[:], components[:], components[:], MULT)
+        amp = held.tile([P, N], F32, name="amp")
+        for h in range(N // BANK):
+            cols = slice(h * BANK, (h + 1) * BANK)
+            sums = psum.tile([P, BANK], F32, name="sums")
+            nc.tensor.matmul(sums[:], ones[:], squares[:, cols], start=True, stop=True)
+            nc.scalar.activation(amp[:, cols], sums[:], SQRT)
+
+        for b in range(blocks):
+            rows = slice(b * P, (b + 1) * P)
+            window = windows.tile([P, S], F32, name="window")
+            nc.sync.dma_start(window[:], table[rows, :])
+            product = products.tile([P, N], F32, name="product")
+            nc.vector.tensor_tensor(product[:], window[:].indirect(offsets[:]), amp[:], MULT)
+            nc.scalar.dma_start(out[rows, :], product[:])

@@ -5,7 +5,7 @@ MULT = mybir.AluOpType.mult
 SQRT = mybir.ActivationFunctionType.Sqrt
 
 P = 128
-BANK = 512
+PIECE = 512
 
 FLOPS = 2 * 128 * 1024 + 1024 * 1024
 
@@ -15,34 +15,38 @@ def tile_omegaentangle_kernel(tc, table, vulns, offs, out):
     C, S = table.shape
     K, N = vulns.shape
     blocks = C // P
+    pieces = N // PIECE
 
     with (
         tc.tile_pool(name="held", bufs=1) as held,
         tc.tile_pool(name="windows", bufs=blocks) as windows,
-        tc.tile_pool(name="products", bufs=blocks) as products,
-        tc.psum_pool(name="psum", bufs=N // BANK) as psum,
+        tc.tile_pool(name="products", bufs=blocks * pieces) as products,
+        tc.psum_pool(name="psum", bufs=pieces) as psum,
     ):
         offsets = held.tile([P, N // 16], U16, name="offsets")
         nc.sync.dma_start(offsets[:], offs)
 
-        components = held.tile([K, N], F32, name="components")
-        nc.scalar.dma_start(components[:], vulns)
+        components = [held.tile([K, PIECE], F32, name=f"components{q}") for q in range(pieces)]
+        for q in range(pieces):
+            nc.scalar.dma_start(components[q][:], vulns[:, q * PIECE : (q + 1) * PIECE])
+
+        window = [windows.tile([P, S], F32, name="window") for b in range(blocks)]
+        for b in range(blocks):
+            nc.sync.dma_start(window[b][:], table[b * P : (b + 1) * P, :])
 
         ones = held.tile([K, P], BF16, name="ones")
         nc.gpsimd.memset(ones[:], 1.0)
-        squares = held.tile([K, N], BF16, name="squares")
-        nc.vector.tensor_tensor(squares[:], components[:], components[:], MULT)
-        amp = held.tile([P, N], F32, name="amp")
-        for h in range(N // BANK):
-            cols = slice(h * BANK, (h + 1) * BANK)
-            sums = psum.tile([P, BANK], F32, name="sums")
-            nc.tensor.matmul(sums[:], ones[:], squares[:, cols], start=True, stop=True)
-            nc.scalar.activation(amp[:, cols], sums[:], SQRT)
+        amp = [held.tile([P, PIECE], F32, name=f"amp{q}") for q in range(pieces)]
+        for q in range(pieces):
+            squares = held.tile([K, PIECE], BF16, name=f"squares{q}")
+            nc.vector.tensor_tensor(squares[:], components[q][:], components[q][:], MULT)
+            sums = psum.tile([P, PIECE], F32, name="sums")
+            nc.tensor.matmul(sums[:], ones[:], squares[:], start=True, stop=True)
+            nc.scalar.activation(amp[q][:], sums[:], SQRT)
 
         for b in range(blocks):
-            rows = slice(b * P, (b + 1) * P)
-            window = windows.tile([P, S], F32, name="window")
-            nc.sync.dma_start(window[:], table[rows, :])
-            product = products.tile([P, N], F32, name="product")
-            nc.vector.tensor_tensor(product[:], window[:].indirect(offsets[:]), amp[:], MULT)
-            nc.scalar.dma_start(out[rows, :], product[:])
+            for q in range(pieces):
+                listed = offsets[:, q * (PIECE // 16) : (q + 1) * (PIECE // 16)]
+                product = products.tile([P, PIECE], F32, name="product")
+                nc.vector.tensor_tensor(product[:], window[b][:].indirect(listed), amp[q][:], MULT)
+                nc.scalar.dma_start(out[b * P : (b + 1) * P, q * PIECE : (q + 1) * PIECE], product[:])

@@ -5,7 +5,7 @@ MULT = mybir.AluOpType.mult
 SQRT = mybir.ActivationFunctionType.Sqrt
 
 P = 128
-PIECE = 512
+PIECE = 256
 
 FLOPS = 2 * 128 * 1024 + 1024 * 1024
 

@@ -20,33 +20,34 @@ def tile_omegaentangle_kernel(tc, table, vulns, offs, out):
     with (
         tc.tile_pool(name="held", bufs=1) as held,
         tc.tile_pool(name="windows", bufs=blocks) as windows,
-        tc.tile_pool(name="products", bufs=blocks * pieces) as products,
+        tc.tile_pool(name="products", bufs=blocks) as products,
         tc.psum_pool(name="psum", bufs=pieces) as psum,
     ):
         offsets = held.tile([P, N // 16], U16, name="offsets")
         nc.sync.dma_start(offsets[:], offs)
-
         components = [held.tile([K, PIECE], F32, name=f"components{q}") for q in range(pieces)]
         for q in range(pieces):
-            nc.scalar.dma_start(components[q][:], vulns[:, q * PIECE : (q + 1) * PIECE])
-
+            nc.sync.dma_start(components[q][:], vulns[:, q * PIECE : (q + 1) * PIECE])
         window = [windows.tile([P, S], F32, name="window") for b in range(blocks)]
         for b in range(blocks):
             nc.sync.dma_start(window[b][:], table[b * P : (b + 1) * P, :])
 
         ones = held.tile([K, P], BF16, name="ones")
         nc.gpsimd.memset(ones[:], 1.0)
-        amp = [held.tile([P, PIECE], F32, name=f"amp{q}") for q in range(pieces)]
+        amp = held.tile([P, N], F32, name="amp")
         for q in range(pieces):
             squares = held.tile([K, PIECE], BF16, name=f"squares{q}")
             nc.vector.tensor_tensor(squares[:], components[q][:], components[q][:], MULT)
             sums = psum.tile([P, PIECE], F32, name="sums")
             nc.tensor.matmul(sums[:], ones[:], squares[:], start=True, stop=True)
-            nc.scalar.activation(amp[q][:], sums[:], SQRT)
+            nc.scalar.activation(amp[:, q * PIECE : (q + 1) * PIECE], sums[:], SQRT)
 
         for b in range(blocks):
-            for q in range(pieces):
-                listed = offsets[:, q * (PIECE // 16) : (q + 1) * (PIECE // 16)]
-                product = products.tile([P, PIECE], F32, name="product")
-                nc.vector.tensor_tensor(product[:], window[b][:].indirect(listed), amp[q][:], MULT)
-                nc.scalar.dma_start(out[b * P : (b + 1) * P, q * PIECE : (q + 1) * PIECE], product[:])
+            product = products.tile([P, N], F32, name="product")
+            step = PIECE if b in (0, blocks - 1) else N
+            for j in range(0, N, step):
+                listed = offsets[:, j // 16 : (j + step) // 16]
+                nc.vector.tensor_tensor(
+                    product[:, j : j + step], window[b][:].indirect(listed), amp[:, j : j + step], MULT
+                )
+                nc.scalar.dma_start(out[b * P : (b + 1) * P, j : j + step], product[:, j : j + step])

@@ -50,4 +50,4 @@ def tile_omegaentangle_kernel(tc, table, vulns, offs, out):
                 nc.vector.tensor_tensor(
                     product[:, j : j + step], window[b][:].indirect(listed), amp[:, j : j + step], MULT
                 )
-                nc.scalar.dma_start(out[b * P : (b + 1) * P, j : j + step], product[:, j : j + step])
+                nc.sync.dma_start(out[b * P : (b + 1) * P, j : j + step], product[:, j : j + step])

@@ -3,9 +3,11 @@ import concourse.mybir as mybir
 F32, BF16, U16 = mybir.dt.float32, mybir.dt.bfloat16, mybir.dt.uint16
 MULT = mybir.AluOpType.mult
 SQRT = mybir.ActivationFunctionType.Sqrt
+SQUARE = mybir.ActivationFunctionType.Square
 
 P = 128
 PIECE = 256
+EARLY = 3
 
 FLOPS = 2 * 128 * 1024 + 1024 * 1024
 
@@ -24,23 +26,42 @@ def tile_omegaentangle_kernel(tc, table, vulns, offs, out):
         tc.psum_pool(name="psum", bufs=pieces) as psum,
     ):
         offsets = held.tile([P, N // 16], U16, name="offsets")
-        nc.sync.dma_start(offsets[:], offs)
         components = [held.tile([K, PIECE], F32, name=f"components{q}") for q in range(pieces)]
-        for q in range(pieces):
-            nc.sync.dma_start(components[q][:], vulns[:, q * PIECE : (q + 1) * PIECE])
         window = [windows.tile([P, S], F32, name="window") for b in range(blocks)]
-        for b in range(blocks):
+
+        def load_components(q):
+            nc.sync.dma_start(components[q][:], vulns[:, q * PIECE : (q + 1) * PIECE])
+
+        for q in range(EARLY):
+            load_components(q)
+        nc.sync.dma_start(offsets[:], offs)
+        nc.sync.dma_start(window[0][:], table[0:P, :])
+        for q in range(EARLY, pieces):
+            load_components(q)
+        for b in range(1, blocks):
             nc.sync.dma_start(window[b][:], table[b * P : (b + 1) * P, :])
 
         ones = held.tile([K, P], BF16, name="ones")
         nc.gpsimd.memset(ones[:], 1.0)
         amp = held.tile([P, N], F32, name="amp")
-        for q in range(pieces):
+        sums = [psum.tile([P, PIECE], F32, name="sums") for q in range(pieces)]
+
+        def square_and_sum(q):
             squares = held.tile([K, PIECE], BF16, name=f"squares{q}")
-            nc.vector.tensor_tensor(squares[:], components[q][:], components[q][:], MULT)
-            sums = psum.tile([P, PIECE], F32, name="sums")
-            nc.tensor.matmul(sums[:], ones[:], squares[:], start=True, stop=True)
-            nc.scalar.activation(amp[:, q * PIECE : (q + 1) * PIECE], sums[:], SQRT)
+            if q < EARLY:
+                nc.vector.tensor_tensor(squares[:], components[q][:], components[q][:], MULT)
+            else:
+                nc.scalar.activation(squares[:], components[q][:], SQUARE)
+            nc.tensor.matmul(sums[q][:], ones[:], squares[:], start=True, stop=True)
+
+        def root(q):
+            nc.scalar.activation(amp[:, q * PIECE : (q + 1) * PIECE], sums[q][:], SQRT)
+
+        for group in (range(EARLY), range(EARLY, pieces)):
+            for q in group:
+                square_and_sum(q)
+            for q in group:
+                root(q)
 
         for b in range(blocks):
             product = products.tile([P, N], F32, name="product")

@@ -7,6 +7,7 @@ SQUARE = mybir.ActivationFunctionType.Square
 
 P = 128
 PIECE = 256
+LAST = 128
 EARLY = 3
 
 FLOPS = 2 * 128 * 1024 + 1024 * 1024
@@ -63,12 +64,21 @@ def tile_omegaentangle_kernel(tc, table, vulns, offs, out):
             for q in group:
                 root(q)
 
+        halving = []
+        left = N
+        while left > LAST:
+            halving.append(left // 2)
+            left -= left // 2
+        halving.append(left)
+        cuts = [[PIECE] * pieces] + [[N]] * (blocks - 2) + [halving]
+
         for b in range(blocks):
             product = products.tile([P, N], F32, name="product")
-            step = PIECE if b in (0, blocks - 1) else N
-            for j in range(0, N, step):
+            j = 0
+            for step in cuts[b]:
                 listed = offsets[:, j // 16 : (j + step) // 16]
                 nc.vector.tensor_tensor(
                     product[:, j : j + step], window[b][:].indirect(listed), amp[:, j : j + step], MULT
                 )
                 nc.sync.dma_start(out[b * P : (b + 1) * P, j : j + step], product[:, j : j + step])
+                j += step

import concourse.mybir as mybir

F32, BF16, U16 = mybir.dt.float32, mybir.dt.bfloat16, mybir.dt.uint16
MULT = mybir.AluOpType.mult
SQRT = mybir.ActivationFunctionType.Sqrt
SQUARE = mybir.ActivationFunctionType.Square

P = 128
PIECE = 256
LAST = 128
EARLY = 3

FLOPS = 2 * 128 * 1024 + 1024 * 1024


def tile_omegaentangle_kernel(tc, table, vulns, offs, out):
    nc = tc.nc
    C, S = table.shape
    K, N = vulns.shape
    blocks = C // P
    pieces = N // PIECE

    with (
        tc.tile_pool(name="held", bufs=1) as held,
        tc.tile_pool(name="windows", bufs=blocks) as windows,
        tc.tile_pool(name="products", bufs=blocks) as products,
        tc.psum_pool(name="psum", bufs=pieces) as psum,
    ):
        offsets = held.tile([P, N // 16], U16, name="offsets")
        components = [held.tile([K, PIECE], F32, name=f"components{q}") for q in range(pieces)]
        window = [windows.tile([P, S], F32, name="window") for b in range(blocks)]

        def load_components(q):
            nc.sync.dma_start(components[q][:], vulns[:, q * PIECE : (q + 1) * PIECE])

        for q in range(EARLY):
            load_components(q)
        nc.sync.dma_start(offsets[:], offs)
        nc.sync.dma_start(window[0][:], table[0:P, :])
        for q in range(EARLY, pieces):
            load_components(q)
        for b in range(1, blocks):
            nc.sync.dma_start(window[b][:], table[b * P : (b + 1) * P, :])

        ones = held.tile([K, P], BF16, name="ones")
        nc.gpsimd.memset(ones[:], 1.0)
        amp = held.tile([P, N], F32, name="amp")
        sums = [psum.tile([P, PIECE], F32, name="sums") for q in range(pieces)]

        def square_and_sum(q):
            squares = held.tile([K, PIECE], BF16, name=f"squares{q}")
            if q < EARLY:
                nc.vector.tensor_tensor(squares[:], components[q][:], components[q][:], MULT)
            else:
                nc.scalar.activation(squares[:], components[q][:], SQUARE)
            nc.tensor.matmul(sums[q][:], ones[:], squares[:], start=True, stop=True)

        def root(q):
            nc.scalar.activation(amp[:, q * PIECE : (q + 1) * PIECE], sums[q][:], SQRT)

        for group in (range(EARLY), range(EARLY, pieces)):
            for q in group:
                square_and_sum(q)
            for q in group:
                root(q)

        halving = []
        left = N
        while left > LAST:
            halving.append(left // 2)
            left -= left // 2
        halving.append(left)
        cuts = [[PIECE] * pieces] + [[N]] * (blocks - 2) + [halving]

        for b in range(blocks):
            product = products.tile([P, N], F32, name="product")
            j = 0
            for step in cuts[b]:
                listed = offsets[:, j // 16 : (j + step) // 16]
                nc.vector.tensor_tensor(
                    product[:, j : j + step], window[b][:].indirect(listed), amp[:, j : j + step], MULT
                )
                nc.sync.dma_start(out[b * P : (b + 1) * P, j : j + step], product[:, j : j + step])
                j += step
